import numpy as np
import ml_dtypes


def mxq(x, axis, fmt="e4m3"):
    dtype, down = {"e4m3": (ml_dtypes.float8_e4m3fn, 7), "e5m2": (ml_dtypes.float8_e5m2, 14)}[fmt]
    v = np.moveaxis(np.asarray(x, np.float32).astype(ml_dtypes.bfloat16).astype(np.float64), axis, -1)
    blocks = v.reshape(v.shape[:-1] + (-1, 32))
    amax = np.abs(blocks).max(-1, keepdims=True)
    byte = np.maximum(np.where(amax > 0, np.frexp(amax)[1] - 1 + 127, 0) - down, 1)
    scale = np.exp2(byte - 127.0)
    codes = (blocks / scale).astype(np.float32).astype(dtype).astype(np.float64)
    return np.moveaxis((codes * scale).reshape(v.shape), -1, axis)


WIDE = False


def mx_kscale(k):
    if not WIDE:
        return np.ones(k)
    levels = np.array([10, -10, 5, -5, 0])
    a = np.random.permutation(np.resize(levels, k // 512 * 4)).reshape(k // 512, 4)
    idx = np.arange(k)
    return np.exp2(a[idx // 512, idx % 128 // 32])


BF16 = ml_dtypes.bfloat16


def bf(x):
    return np.asarray(x, np.float32).astype(BF16)


def f64(x):
    return np.asarray(x).astype(np.float64)


N, IN, OUT, R, KD, K = 512, 2048, 2048, 32, 32, 16
KR = K * R
GATE_THRESHOLD = 0.05


def setup_inputs():
    s, t = mx_kscale(IN), mx_kscale(KR)
    tk = t.reshape(K, R)
    return {"x": bf(np.random.standard_normal((N, IN)) * s),
            "scores": bf(np.random.standard_normal((N, K))),
            "Wb": bf(np.random.standard_normal((OUT, IN)) / np.sqrt(IN) / s),
            "bb": bf(np.random.standard_normal(OUT) * 0.3),
            "A": bf(np.random.standard_normal((K, OUT, R)) * 2.0 / np.sqrt(R) / tk[:, None, :]),
            "B": bf(np.random.standard_normal((K, R, IN)) / np.sqrt(IN) / s * tk[:, :, None])}


def reference(x, scores, Wb, bb, A, B):
    xq = mxq(f64(x), 1, "e4m3")
    base = (xq @ mxq(f64(Wb), 1, "e4m3").T) + f64(bb)
    sc = f64(scores)
    e = np.exp(sc - sc.max(-1, keepdims=True))
    g = e / e.sum(-1, keepdims=True)
    g = np.where(g > GATE_THRESHOLD, g, 0.0)
    g = g / np.maximum(g.sum(-1, keepdims=True), 1e-8)
    u = xq @ mxq(f64(B).reshape(KR, IN), 1, "e4m3").T
    h = (g[:, :, None] * u.reshape(N, K, R)).reshape(N, KR)
    Af = f64(A).transpose(0, 2, 1).reshape(KR, OUT)
    delta = mxq(h, 1, "e4m3") @ mxq(Af, 0, "e4m3")
    return base + delta

@@ -1,0 +1,264 @@
+from contextlib import ExitStack
+
+import concourse.mybir as mybir
+from concourse.masks import make_identity
+
+F32 = mybir.dt.float32
+BF16 = mybir.dt.bfloat16
+U32 = mybir.dt.uint32
+U8 = mybir.dt.uint8
+FP8X4 = mybir.dt.float8_e4m3fn_x4
+ALU = mybir.AluOpType
+ACT = mybir.ActivationFunctionType
+AX = mybir.AxisListType
+
+P = 128
+N_TOK = 512
+D_IN = 2048
+D_OUT = 2048
+N_EXP = 16
+RANK = 32
+KR = N_EXP * RANK
+NB = N_TOK // P
+G = D_IN // 512
+MC = D_OUT // 512
+GATE_THRESHOLD = 0.05
+
+FLOPS = 2 * N_TOK * D_IN * D_OUT + 2 * N_TOK * D_IN * KR + 2 * N_TOK * KR * D_OUT
+
+
+def tile_submatrixlinear_pa_kernel(tc, x, scores, Wb, bb, A, B, out):
+    nc = tc.nc
+    with ExitStack() as ctx:
+        const = ctx.enter_context(tc.tile_pool(name="const", bufs=1))
+        raw = ctx.enter_context(tc.tile_pool(name="raw", bufs=16))
+        grp = ctx.enter_context(tc.tile_pool(name="grp", bufs=3))
+        outp = ctx.enter_context(tc.tile_pool(name="outp", bufs=6))
+        small = ctx.enter_context(tc.tile_pool(name="small", bufs=1))
+        tps = ctx.enter_context(tc.psum_pool(name="tps", bufs=4))
+        accs = ctx.enter_context(tc.psum_pool(name="accs", bufs=4))
+
+        ident = const.tile([P, P], F32, name="ident")
+        make_identity(nc, ident[:])
+        ones = const.tile([P, P], BF16, name="ones")
+        nc.vector.memset(ones[:], 1.0)
+        bias_row = raw.tile([P, D_OUT], BF16, name="bias_row", tag="raw")
+        nc.vector.memset(bias_row[:], 0.0)
+
+        bias_sb = const.tile([P, D_OUT], F32, name="bias_sb")
+        a_raw = const.tile([P, MC, 2048], BF16, name="a_raw", align_bytes=64)
+        xq = const.tile([P, NB, G, P], U32, name="xq", align_bytes=64)
+        xs = const.tile([P, NB, G, P], U8, name="xs", align_bytes=64)
+        bq = const.tile([P, 4, G, P], U32, name="bq", align_bytes=64)
+        bs = const.tile([P, 4, G, P], U8, name="bs", align_bytes=64)
+        wq = const.tile([P, MC, G, 512], U32, name="wq", align_bytes=64)
+        ws = const.tile([P, MC, G, 512], U8, name="ws", align_bytes=64)
+        aq = const.tile([P, MC, 512], U32, name="aq", align_bytes=64)
+        asc = const.tile([P, MC, 512], U8, name="asc", align_bytes=64)
+        hq = const.tile([P, NB, P], U32, name="hq", align_bytes=64)
+        hs = const.tile([P, NB, P], U8, name="hs", align_bytes=64)
+        hg = const.tile([P, NB, P, 4], BF16, name="hg", align_bytes=64)
+
+        sc_b = small.tile([P, NB, N_EXP], BF16, name="sc_b")
+        nc.sync.dma_start(out=sc_b[:], in_=scores.rearrange("(c p) k -> p c k", p=P))
+        nc.sync.dma_start(out=bias_row[0:1, :], in_=bb.rearrange("(o n) -> o n", o=1))
+
+        def load_rows(src, r0, nm):
+            t = raw.tile([P, D_IN], BF16, name=nm, tag="raw")
+            nc.sync.dma_start(out=t[:], in_=src[r0 : r0 + P, :])
+            return t
+
+        Bf = B.rearrange("k r i -> (k r) i")
+        x_raw = [load_rows(x, P * i, "x_raw%d" % i) for i in range(NB)]
+        b_raw = [load_rows(Bf, P * i, "b_raw%d" % i) for i in range(4)]
+        w_raw = [load_rows(Wb, P * i, "w_raw%d" % i) for i in range(4)]
+        for k in range(N_EXP):
+            t, a = k // 4, k % 4
+            nc.sync.dma_start(
+                out=a_raw[32 * a + t : 32 * a + 32 : 4, :, :],
+                in_=A[k].rearrange("(m i b) r -> i m (b r)", m=MC, i=8, b=64),
+            )
+        for i in range(4, 16):
+            w_raw.append(load_rows(Wb, P * i, "w_raw%d" % i))
+
+        mx = small.tile([P, NB], F32, name="mx")
+        nc.vector.tensor_reduce(out=mx[:], in_=sc_b[:], axis=AX.X, op=ALU.max)
+        dif = small.tile([P, NB, N_EXP], F32, name="dif")
+        nc.vector.tensor_tensor(
+            out=dif[:], in0=sc_b[:], in1=mx[:].unsqueeze(2).to_broadcast([P, NB, N_EXP]), op=ALU.subtract
+        )
+        ex = small.tile([P, NB, N_EXP], F32, name="ex")
+        nc.scalar.activation(out=ex[:], in_=dif[:], func=ACT.Exp)
+        sm = small.tile([P, NB], F32, name="sm")
+        nc.vector.tensor_reduce(out=sm[:], in_=ex[:], axis=AX.X, op=ALU.add)
+        rs = small.tile([P, NB], F32, name="rs")
+        nc.vector.reciprocal(out=rs[:], in_=sm[:])
+        g0 = small.tile([P, NB, N_EXP], F32, name="g0")
+        nc.vector.tensor_tensor(
+            out=g0[:], in0=ex[:], in1=rs[:].unsqueeze(2).to_broadcast([P, NB, N_EXP]), op=ALU.mult
+        )
+        g1 = small.tile([P, NB, N_EXP], F32, name="g1")
+        nc.vector.scalar_tensor_tensor(
+            out=g1[:].rearrange("p c k -> p (c k)"),
+            in0=g0[:].rearrange("p c k -> p (c k)"),
+            scalar=GATE_THRESHOLD,
+            in1=g0[:].rearrange("p c k -> p (c k)"),
+            op0=ALU.is_gt,
+            op1=ALU.mult,
+        )
+        s1 = small.tile([P, NB], F32, name="s1")
+        nc.vector.tensor_reduce(out=s1[:], in_=g1[:], axis=AX.X, op=ALU.add)
+        s1m = small.tile([P, NB], F32, name="s1m")
+        nc.vector.tensor_scalar_max(out=s1m[:], in0=s1[:], scalar1=1e-8)
+        r1 = small.tile([P, NB], F32, name="r1")
+        nc.vector.reciprocal(out=r1[:], in_=s1m[:])
+
+        for m in range(MC):
+            pb = accs.tile([P, 512], F32, name="pb", tag="acc")
+            nc.tensor.matmul(out=pb[:], lhsT=ones[:], rhs=bias_row[:, 512 * m : 512 * m + 512], start=True, stop=True)
+            nc.scalar.copy(out=bias_sb[:, 512 * m : 512 * m + 512], in_=pb[:])
+
+        def rows_to_codes(src, codes, scales):
+            words = src[:].bitcast(F32)
+            gx = grp.tile([P, 2048], BF16, name="gx", tag="gx", align_bytes=64)
+            gxw = gx[:].bitcast(F32).rearrange("p (g n u) -> p g n u", g=G, n=P, u=2)
+            for gp in range(2):
+                bank = tps.tile([P, 4, P], F32, name="bank", tag="tp")
+                for g2 in range(2):
+                    for u in range(2):
+                        c0 = 256 * (2 * gp + g2) + 128 * u
+                        nc.tensor.transpose(bank[:, 2 * g2 + u, :], words[:, c0 : c0 + P], ident[:])
+                nc.scalar.copy(
+                    out=gxw[:, 2 * gp : 2 * gp + 2],
+                    in_=bank[:].rearrange("p (g u) n -> p g n u", u=2),
+                )
+            nc.vector.quantize_mx(
+                out=codes.rearrange("p g n -> p (g n)").bitcast(FP8X4),
+                scales=scales.rearrange("p g n -> p (g n)"),
+                in_=gx[:],
+            )
+
+        for nb in range(NB):
+            rows_to_codes(x_raw[nb], xq[:, nb], xs[:, nb])
+
+        gts = []
+        for nb in range(NB):
+            gexp = outp.tile([P, 512], F32, name="gexp", tag="o")
+            nc.vector.tensor_scalar(
+                out=gexp[:].rearrange("p (k r) -> p k r", r=RANK),
+                in0=g1[:, nb, :].unsqueeze(2).to_broadcast([P, N_EXP, RANK]),
+                scalar1=r1[:, nb : nb + 1],
+                scalar2=None,
+                op0=ALU.mult,
+            )
+            bank = tps.tile([P, 4, P], F32, name="bank", tag="tp")
+            for t in range(4):
+                nc.tensor.transpose(bank[:, t, :], gexp[:, P * t : P * t + P], ident[:])
+            gt = outp.tile([P, 512], F32, name="gt", tag="o")
+            nc.scalar.copy(
+                out=gt[:].rearrange("p (n t) -> p n t", t=4), in_=bank[:].rearrange("p t n -> p n t")
+            )
+            gts.append(gt)
+
+        for t in range(4):
+            rows_to_codes(b_raw[t], bq[:, t], bs[:, t])
+
+        ut = [accs.tile([P, 4, P], F32, name="ut%d" % nb, tag="acc") for nb in range(NB)]
+        for t in range(4):
+            for nb in range(NB):
+                for g in range(G):
+                    nc.tensor.matmul_mx(
+                        out=ut[nb][:, t, :],
+                        lhsT=bq[:, t, g, :].bitcast(FP8X4),
+                        lhsT_scale=bs[:, t, g, :],
+                        rhs=xq[:, nb, g, :].bitcast(FP8X4),
+                        rhs_scale=xs[:, nb, g, :],
+                        start=(g == 0),
+                        stop=(g == G - 1),
+                    )
+        for nb in range(NB):
+            nc.vector.tensor_tensor(
+                out=hg[:, nb],
+                in0=ut[nb][:].rearrange("p t n -> p n t"),
+                in1=gts[nb][:].rearrange("p (n t) -> p n t", t=4),
+                op=ALU.mult,
+            )
+        for nb in range(NB):
+            nc.vector.quantize_mx(
+                out=hq[:, nb, :].bitcast(FP8X4),
+                scales=hs[:, nb, :],
+                in_=hg[:, nb].rearrange("p n t -> p (n t)"),
+            )
+
+        def a_chunk(m):
+            y = grp.tile([P, 2048], BF16, name="y", tag="y", bufs=2, align_bytes=64)
+            nc.vector.transpose(out=y[:], in_=a_raw[:, m, :])
+            nc.vector.quantize_mx(out=aq[:, m, :].bitcast(FP8X4), scales=asc[:, m, :], in_=y[:])
+
+        def w_transposes(m, half, wgs):
+            for g in range(G):
+                bank = tps.tile([P, 4, P], F32, name="bank", tag="tp")
+                for u in range(2):
+                    for jj in range(2):
+                        words = w_raw[4 * m + 2 * half + jj][:].bitcast(F32)
+                        c0 = 256 * g + 128 * u
+                        nc.tensor.transpose(bank[:, 2 * u + jj, :], words[:, c0 : c0 + P], ident[:])
+                nc.scalar.copy(
+                    out=wgs[g][:].bitcast(F32).rearrange("p (b h s u) -> p h b s u", b=64, h=2, s=4, u=2)[:, half],
+                    in_=bank[:].rearrange("p a q -> p (a q)").rearrange("p (u s b) -> p b s u", u=2, s=4, b=64),
+                )
+
+        def w_quantise(m, wgs):
+            for g in range(G):
+                nc.vector.quantize_mx(out=wq[:, m, g, :].bitcast(FP8X4), scales=ws[:, m, g, :], in_=wgs[g][:])
+
+        def w_tiles():
+            return [grp.tile([P, 2048], BF16, name="wg%d" % g, tag="wg", bufs=6, align_bytes=64) for g in range(G)]
+
+        def mx_block(m, nb):
+            acc = accs.tile([P, 512], F32, name="acc", tag="acc")
+            for g in range(G):
+                nc.tensor.matmul_mx(
+                    out=acc[:],
+                    lhsT=xq[:, nb, g, :].bitcast(FP8X4),
+                    lhsT_scale=xs[:, nb, g, :],
+                    rhs=wq[:, m, g, :].bitcast(FP8X4),
+                    rhs_scale=ws[:, m, g, :],
+                    start=(g == 0),
+                    stop=False,
+                )
+            nc.tensor.matmul_mx(
+                out=acc[:],
+                lhsT=hq[:, nb, :].bitcast(FP8X4),
+                lhsT_scale=hs[:, nb, :],
+                rhs=aq[:, m, :].bitcast(FP8X4),
+                rhs_scale=asc[:, m, :],
+                start=False,
+                stop=True,
+            )
+            o = outp.tile([P, 512], F32, name="o", tag="o")
+            nc.vector.tensor_tensor(
+                out=o[:].rearrange("p (i b) -> p i b", i=8),
+                in0=acc[:].rearrange("p (b i) -> p i b", i=8),
+                in1=bias_sb[:, 512 * m : 512 * m + 512].rearrange("p (i b) -> p i b", i=8),
+                op=ALU.add,
+            )
+            nc.sync.dma_start(out=out[P * nb : P * nb + P, 512 * m : 512 * m + 512], in_=o[:])
+
+        wgs = w_tiles()
+        w_transposes(0, 0, wgs)
+        w_transposes(0, 1, wgs)
+        w_quantise(0, wgs)
+        a_chunk(0)
+        for m in range(MC):
+            nxt = w_tiles() if m + 1 < MC else None
+            if nxt is not None:
+                w_transposes(m + 1, 0, nxt)
+            mx_block(m, 0)
+            mx_block(m, 1)
+            if nxt is not None:
+                w_transposes(m + 1, 1, nxt)
+                w_quantise(m + 1, nxt)
+                a_chunk(m + 1)
+            mx_block(m, 2)
+            mx_block(m, 3)

@@ -27,16 +27,22 @@ GATE_THRESHOLD = 0.05
 FLOPS = 2 * N_TOK * D_IN * D_OUT + 2 * N_TOK * D_IN * KR + 2 * N_TOK * KR * D_OUT
 
 
+PIN = True
+A_ON_GPSIMD = False
+
+
 def tile_submatrixlinear_pa_kernel(tc, x, scores, Wb, bb, A, B, out):
     nc = tc.nc
     with ExitStack() as ctx:
         const = ctx.enter_context(tc.tile_pool(name="const", bufs=1))
-        raw = ctx.enter_context(tc.tile_pool(name="raw", bufs=16))
+        raw = ctx.enter_context(tc.tile_pool(name="raw", bufs=12))
         grp = ctx.enter_context(tc.tile_pool(name="grp", bufs=3))
         outp = ctx.enter_context(tc.tile_pool(name="outp", bufs=6))
         small = ctx.enter_context(tc.tile_pool(name="small", bufs=1))
         tps = ctx.enter_context(tc.psum_pool(name="tps", bufs=4))
         accs = ctx.enter_context(tc.psum_pool(name="accs", bufs=4))
+        if PIN:
+            ctx.enter_context(tc.manual_schedule())
 
         ident = const.tile([P, P], F32, name="ident")
         make_identity(nc, ident[:])
@@ -44,6 +50,10 @@ def tile_submatrixlinear_pa_kernel(tc, x, scores, Wb, bb, A, B, out):
         nc.vector.memset(ones[:], 1.0)
         bias_row = raw.tile([P, D_OUT], BF16, name="bias_row", tag="raw")
         nc.vector.memset(bias_row[:], 0.0)
+        perm = const.tile([P, P], F32, name="perm")
+        nc.vector.tensor_copy(
+            out=perm[:].rearrange("p (b s) -> p b s", s=2), in_=ident[:].rearrange("p (s b) -> p b s", s=2)
+        )
 
         bias_sb = const.tile([P, D_OUT], F32, name="bias_sb")
         a_raw = const.tile([P, MC, 2048], BF16, name="a_raw", align_bytes=64)
@@ -68,16 +78,24 @@ def tile_submatrixlinear_pa_kernel(tc, x, scores, Wb, bb, A, B, out):
             nc.sync.dma_start(out=t[:], in_=src[r0 : r0 + P, :])
             return t
 
+        a_queue = nc.gpsimd if A_ON_GPSIMD else nc.sync
+
+        def load_a():
+            for k in range(N_EXP):
+                t, a = k // 4, k % 4
+                a_queue.dma_start(
+                    out=a_raw[32 * a + t : 32 * a + 32 : 4, :, :],
+                    in_=A[k].rearrange("(m i b) r -> i m (b r)", m=MC, i=8, b=64),
+                )
+
         Bf = B.rearrange("k r i -> (k r) i")
+        if A_ON_GPSIMD:
+            load_a()
         x_raw = [load_rows(x, P * i, "x_raw%d" % i) for i in range(NB)]
         b_raw = [load_rows(Bf, P * i, "b_raw%d" % i) for i in range(4)]
         w_raw = [load_rows(Wb, P * i, "w_raw%d" % i) for i in range(4)]
-        for k in range(N_EXP):
-            t, a = k // 4, k % 4
-            nc.sync.dma_start(
-                out=a_raw[32 * a + t : 32 * a + 32 : 4, :, :],
-                in_=A[k].rearrange("(m i b) r -> i m (b r)", m=MC, i=8, b=64),
-            )
+        if not A_ON_GPSIMD:
+            load_a()
         for i in range(4, 16):
             w_raw.append(load_rows(Wb, P * i, "w_raw%d" % i))
 
@@ -112,6 +130,17 @@ def tile_submatrixlinear_pa_kernel(tc, x, scores, Wb, bb, A, B, out):
         nc.vector.tensor_scalar_max(out=s1m[:], in0=s1[:], scalar1=1e-8)
         r1 = small.tile([P, NB], F32, name="r1")
         nc.vector.reciprocal(out=r1[:], in_=s1m[:])
+        gexps = []
+        for nb in range(NB):
+            gexp = outp.tile([P, 512], F32, name="gexp", tag="o")
+            nc.vector.tensor_scalar(
+                out=gexp[:].rearrange("p (k r) -> p k r", r=RANK),
+                in0=g1[:, nb, :].unsqueeze(2).to_broadcast([P, N_EXP, RANK]),
+                scalar1=r1[:, nb : nb + 1],
+                scalar2=None,
+                op0=ALU.mult,
+            )
+            gexps.append(gexp)
 
         for m in range(MC):
             pb = accs.tile([P, 512], F32, name="pb", tag="acc")
@@ -138,84 +167,53 @@ def tile_submatrixlinear_pa_kernel(tc, x, scores, Wb, bb, A, B, out):
                 in_=gx[:],
             )
 
-        for nb in range(NB):
-            rows_to_codes(x_raw[nb], xq[:, nb], xs[:, nb])
-
-        gts = []
-        for nb in range(NB):
-            gexp = outp.tile([P, 512], F32, name="gexp", tag="o")
-            nc.vector.tensor_scalar(
-                out=gexp[:].rearrange("p (k r) -> p k r", r=RANK),
-                in0=g1[:, nb, :].unsqueeze(2).to_broadcast([P, N_EXP, RANK]),
-                scalar1=r1[:, nb : nb + 1],
-                scalar2=None,
-                op0=ALU.mult,
-            )
-            bank = tps.tile([P, 4, P], F32, name="bank", tag="tp")
-            for t in range(4):
-                nc.tensor.transpose(bank[:, t, :], gexp[:, P * t : P * t + P], ident[:])
-            gt = outp.tile([P, 512], F32, name="gt", tag="o")
-            nc.scalar.copy(
-                out=gt[:].rearrange("p (n t) -> p n t", t=4), in_=bank[:].rearrange("p t n -> p n t")
-            )
-            gts.append(gt)
-
-        for t in range(4):
-            rows_to_codes(b_raw[t], bq[:, t], bs[:, t])
-
-        ut = [accs.tile([P, 4, P], F32, name="ut%d" % nb, tag="acc") for nb in range(NB)]
-        for t in range(4):
-            for nb in range(NB):
-                for g in range(G):
-                    nc.tensor.matmul_mx(
-                        out=ut[nb][:, t, :],
-                        lhsT=bq[:, t, g, :].bitcast(FP8X4),
-                        lhsT_scale=bs[:, t, g, :],
-                        rhs=xq[:, nb, g, :].bitcast(FP8X4),
-                        rhs_scale=xs[:, nb, g, :],
-                        start=(g == 0),
-                        stop=(g == G - 1),
-                    )
-        for nb in range(NB):
-            nc.vector.tensor_tensor(
-                out=hg[:, nb],
-                in0=ut[nb][:].rearrange("p t n -> p n t"),
-                in1=gts[nb][:].rearrange("p (n t) -> p n t", t=4),
-                op=ALU.mult,
-            )
-        for nb in range(NB):
-            nc.vector.quantize_mx(
-                out=hq[:, nb, :].bitcast(FP8X4),
-                scales=hs[:, nb, :],
-                in_=hg[:, nb].rearrange("p n t -> p (n t)"),
-            )
+        def ut_passes(ut, t, nb):
+            for g in range(G):
+                nc.tensor.matmul_mx(
+                    out=ut[nb][:, t, :],
+                    lhsT=bq[:, t, g, :].bitcast(FP8X4),
+                    lhsT_scale=bs[:, t, g, :],
+                    rhs=xq[:, nb, g, :].bitcast(FP8X4),
+                    rhs_scale=xs[:, nb, g, :],
+                    start=(g == 0),
+                    stop=(g == G - 1),
+                )
 
         def a_chunk(m):
             y = grp.tile([P, 2048], BF16, name="y", tag="y", bufs=2, align_bytes=64)
             nc.vector.transpose(out=y[:], in_=a_raw[:, m, :])
             nc.vector.quantize_mx(out=aq[:, m, :].bitcast(FP8X4), scales=asc[:, m, :], in_=y[:])
 
-        def w_transposes(m, half, wgs):
-            for g in range(G):
+        def w_block(m, j, wg):
+            words = w_raw[4 * m + j][:].bitcast(F32)
+            wgw = wg[:].bitcast(F32).rearrange("p (g b j s u) -> p j g b s u", g=G, b=64, j=4, s=2, u=2)
+            for gp in range(2):
                 bank = tps.tile([P, 4, P], F32, name="bank", tag="tp")
-                for u in range(2):
-                    for jj in range(2):
-                        words = w_raw[4 * m + 2 * half + jj][:].bitcast(F32)
-                        c0 = 256 * g + 128 * u
-                        nc.tensor.transpose(bank[:, 2 * u + jj, :], words[:, c0 : c0 + P], ident[:])
-                nc.scalar.copy(
-                    out=wgs[g][:].bitcast(F32).rearrange("p (b h s u) -> p h b s u", b=64, h=2, s=4, u=2)[:, half],
-                    in_=bank[:].rearrange("p a q -> p (a q)").rearrange("p (u s b) -> p b s u", u=2, s=4, b=64),
+                for g2 in range(2):
+                    for u in range(2):
+                        c0 = 256 * (2 * gp + g2) + 128 * u
+                        nc.tensor.transpose(bank[:, 2 * g2 + u, :], words[:, c0 : c0 + P], perm[:])
+                for g2 in range(2):
+                    nc.scalar.copy(
+                        out=wgw[:, j, 2 * gp + g2],
+                        in_=bank[:, 2 * g2 : 2 * g2 + 2, :].rearrange("p u (b s) -> p b s u", s=2),
+                    )
+
+        def w_half(m, half, wg):
+            w_block(m, 2 * half, wg)
+            w_block(m, 2 * half + 1, wg)
+
+        def w_quantise(m, wg):
+            for g in range(G):
+                nc.vector.quantize_mx(
+                    out=wq[:, m, g, :].bitcast(FP8X4), scales=ws[:, m, g, :], in_=wg[:, 2048 * g : 2048 * g + 2048]
                 )
 
-        def w_quantise(m, wgs):
-            for g in range(G):
-                nc.vector.quantize_mx(out=wq[:, m, g, :].bitcast(FP8X4), scales=ws[:, m, g, :], in_=wgs[g][:])
+        def w_tile():
+            wg = grp.tile([P, G * 2048], BF16, name="wg", tag="wg", bufs=2, align_bytes=64)
+            return wg
 
-        def w_tiles():
-            return [grp.tile([P, 2048], BF16, name="wg%d" % g, tag="wg", bufs=6, align_bytes=64) for g in range(G)]
-
-        def mx_block(m, nb):
+        def base(m, nb):
             acc = accs.tile([P, 512], F32, name="acc", tag="acc")
             for g in range(G):
                 nc.tensor.matmul_mx(
@@ -227,6 +225,9 @@ def tile_submatrixlinear_pa_kernel(tc, x, scores, Wb, bb, A, B, out):
                     start=(g == 0),
                     stop=False,
                 )
+            return acc
+
+        def delta(m, nb, acc):
             nc.tensor.matmul_mx(
                 out=acc[:],
                 lhsT=hq[:, nb, :].bitcast(FP8X4),
@@ -236,6 +237,8 @@ def tile_submatrixlinear_pa_kernel(tc, x, scores, Wb, bb, A, B, out):
                 start=False,
                 stop=True,
             )
+
+        def finish(m, nb, acc):
             o = outp.tile([P, 512], F32, name="o", tag="o")
             nc.vector.tensor_tensor(
                 out=o[:].rearrange("p (i b) -> p i b", i=8),
@@ -245,20 +248,81 @@ def tile_submatrixlinear_pa_kernel(tc, x, scores, Wb, bb, A, B, out):
             )
             nc.sync.dma_start(out=out[P * nb : P * nb + P, 512 * m : 512 * m + 512], in_=o[:])
 
-        wgs = w_tiles()
-        w_transposes(0, 0, wgs)
-        w_transposes(0, 1, wgs)
-        w_quantise(0, wgs)
+        for nb in range(NB):
+            rows_to_codes(x_raw[nb], xq[:, nb], xs[:, nb])
+
+        gts = []
+        for nb in range(NB):
+            bank = tps.tile([P, 4, P], F32, name="bank", tag="tp")
+            for t in range(4):
+                nc.tensor.transpose(bank[:, t, :], gexps[nb][:, P * t : P * t + P], ident[:])
+            gt = outp.tile([P, 512], F32, name="gt", tag="o")
+            nc.scalar.copy(
+                out=gt[:].rearrange("p (n t) -> p n t", t=4), in_=bank[:].rearrange("p t n -> p n t")
+            )
+            gts.append(gt)
+
+        for t in range(3):
+            rows_to_codes(b_raw[t], bq[:, t], bs[:, t])
+        ut = [accs.tile([P, 4, P], F32, name="ut%d" % nb, tag="acc") for nb in range(NB)]
+        for nb in range(NB):
+            ut_passes(ut, 0, nb)
+        rows_to_codes(b_raw[3], bq[:, 3], bs[:, 3])
+        wg = w_tile()
+        w_half(0, 0, wg)
+        for nb in range(NB):
+            ut_passes(ut, 1, nb)
+        for nb in range(NB):
+            ut_passes(ut, 2, nb)
+        w_half(0, 1, wg)
+
+        def h_block(nb):
+            nc.vector.tensor_tensor(
+                out=hg[:, nb],
+                in0=ut[nb][:].rearrange("p t n -> p n t"),
+                in1=gts[nb][:].rearrange("p (n t) -> p n t", t=4),
+                op=ALU.mult,
+            )
+
+        for nb in range(NB):
+            ut_passes(ut, 3, nb)
+        h_block(0)
+        w_quantise(0, wg)
+        for nb in range(1, NB):
+            h_block(nb)
+        nc.vector.quantize_mx(
+            out=hq[:].rearrange("p c n -> p (c n)").bitcast(FP8X4),
+            scales=hs[:].rearrange("p c n -> p (c n)"),
+            in_=hg[:].rearrange("p c n t -> p (c n t)"),
+        )
+
+        accl = [base(0, nb) for nb in range(NB)]
         a_chunk(0)
-        for m in range(MC):
-            nxt = w_tiles() if m + 1 < MC else None
-            if nxt is not None:
-                w_transposes(m + 1, 0, nxt)
-            mx_block(m, 0)
-            mx_block(m, 1)
-            if nxt is not None:
-                w_transposes(m + 1, 1, nxt)
-                w_quantise(m + 1, nxt)
+        wg = w_tile()
+        w_half(1, 0, wg)
+        for nb in range(NB):
+            delta(0, nb, accl[nb])
+        for nb in range(NB):
+            finish(0, nb, accl[nb])
+        w_half(1, 1, wg)
+        w_quantise(1, wg)
+        a_chunk(1)
+
+        for m in range(1, MC):
+            more = m + 1 < MC
+            if more:
+                wg = w_tile()
+                w_half(m + 1, 0, wg)
+            accl = [base(m, 0), base(m, 1)]
+            if more:
+                w_half(m + 1, 1, wg)
+            accl.append(base(m, 2))
+            accl.append(base(m, 3))
+            for nb in range(NB):
+                delta(m, nb, accl[nb])
+            if more:
+                w_quantise(m + 1, wg)
+            for nb in range(NB):
+                finish(m, nb, accl[nb])
+            if more:
                 a_chunk(m + 1)
-            mx_block(m, 2)
-            mx_block(m, 3)

@@ -29,6 +29,7 @@ FLOPS = 2 * N_TOK * D_IN * D_OUT + 2 * N_TOK * D_IN * KR + 2 * N_TOK * KR * D_OU
 
 PIN = True
 A_ON_GPSIMD = False
+OUT_REGIONS = 4
 
 
 def tile_submatrixlinear_pa_kernel(tc, x, scores, Wb, bb, A, B, out):
@@ -240,12 +241,16 @@ def tile_submatrixlinear_pa_kernel(tc, x, scores, Wb, bb, A, B, out):
 
         def finish(m, nb, acc):
             o = outp.tile([P, 512], F32, name="o", tag="o")
-            nc.vector.tensor_tensor(
-                out=o[:].rearrange("p (i b) -> p i b", i=8),
-                in0=acc[:].rearrange("p (b i) -> p i b", i=8),
-                in1=bias_sb[:, 512 * m : 512 * m + 512].rearrange("p (i b) -> p i b", i=8),
-                op=ALU.add,
-            )
+            ov = o[:].rearrange("p (i b) -> p b i", i=8)
+            av = acc[:].rearrange("p (b i) -> p b i", i=8)
+            bv = bias_sb[:, 512 * m : 512 * m + 512].rearrange("p (i b) -> p b i", i=8)
+            for i0 in range(0, 8, OUT_REGIONS):
+                nc.vector.tensor_tensor(
+                    out=ov[:, :, i0 : i0 + OUT_REGIONS],
+                    in0=av[:, :, i0 : i0 + OUT_REGIONS],
+                    in1=bv[:, :, i0 : i0 + OUT_REGIONS],
+                    op=ALU.add,
+                )
             nc.sync.dma_start(out=out[P * nb : P * nb + P, 512 * m : 512 * m + 512], in_=o[:])
 
         for nb in range(NB):

@@ -28,7 +28,6 @@ FLOPS = 2 * N_TOK * D_IN * D_OUT + 2 * N_TOK * D_IN * KR + 2 * N_TOK * KR * D_OU
 
 
 PIN = True
-A_ON_GPSIMD = False
 OUT_REGIONS = 4
 
 
@@ -38,7 +37,7 @@ def tile_submatrixlinear_pa_kernel(tc, x, scores, Wb, bb, A, B, out):
         const = ctx.enter_context(tc.tile_pool(name="const", bufs=1))
         raw = ctx.enter_context(tc.tile_pool(name="raw", bufs=12))
         grp = ctx.enter_context(tc.tile_pool(name="grp", bufs=3))
-        outp = ctx.enter_context(tc.tile_pool(name="outp", bufs=6))
+        outp = ctx.enter_context(tc.tile_pool(name="outp", bufs=8))
         small = ctx.enter_context(tc.tile_pool(name="small", bufs=1))
         tps = ctx.enter_context(tc.psum_pool(name="tps", bufs=4))
         accs = ctx.enter_context(tc.psum_pool(name="accs", bufs=4))
@@ -51,10 +50,6 @@ def tile_submatrixlinear_pa_kernel(tc, x, scores, Wb, bb, A, B, out):
         nc.vector.memset(ones[:], 1.0)
         bias_row = raw.tile([P, D_OUT], BF16, name="bias_row", tag="raw")
         nc.vector.memset(bias_row[:], 0.0)
-        perm = const.tile([P, P], F32, name="perm")
-        nc.vector.tensor_copy(
-            out=perm[:].rearrange("p (b s) -> p b s", s=2), in_=ident[:].rearrange("p (s b) -> p b s", s=2)
-        )
 
         bias_sb = const.tile([P, D_OUT], F32, name="bias_sb")
         a_raw = const.tile([P, MC, 2048], BF16, name="a_raw", align_bytes=64)
@@ -70,35 +65,39 @@ def tile_submatrixlinear_pa_kernel(tc, x, scores, Wb, bb, A, B, out):
         hs = const.tile([P, NB, P], U8, name="hs", align_bytes=64)
         hg = const.tile([P, NB, P, 4], BF16, name="hg", align_bytes=64)
 
+        xv = x.rearrange("(p c) i -> c p i", c=NB)
+        outv = out.rearrange("(p c) (i m b) -> c m p i b", c=NB, i=8, m=MC, b=64)
+        Bf = B.rearrange("k r i -> (k r) i")
         sc_b = small.tile([P, NB, N_EXP], BF16, name="sc_b")
-        nc.sync.dma_start(out=sc_b[:], in_=scores.rearrange("(c p) k -> p c k", p=P))
+        nc.sync.dma_start(out=sc_b[:], in_=scores.rearrange("(p c) k -> p c k", c=NB))
         nc.sync.dma_start(out=bias_row[0:1, :], in_=bb.rearrange("(o n) -> o n", o=1))
 
-        def load_rows(src, r0, nm):
+        def load_rows(src, nm):
             t = raw.tile([P, D_IN], BF16, name=nm, tag="raw")
-            nc.sync.dma_start(out=t[:], in_=src[r0 : r0 + P, :])
+            nc.sync.dma_start(out=t[:], in_=src)
             return t
 
-        a_queue = nc.gpsimd if A_ON_GPSIMD else nc.sync
+        def load_w(m, j):
+            t = raw.tile([P, D_IN], BF16, name="w_raw", tag="raw")
+            for s in range(2):
+                r0 = 256 * (2 * j + s) + 64 * m
+                nc.sync.dma_start(out=t[s:P:2, :], in_=Wb[r0 : r0 + 64, :])
+            return t
 
-        def load_a():
-            for k in range(N_EXP):
-                t, a = k // 4, k % 4
-                a_queue.dma_start(
-                    out=a_raw[32 * a + t : 32 * a + 32 : 4, :, :],
-                    in_=A[k].rearrange("(m i b) r -> i m (b r)", m=MC, i=8, b=64),
+        def load_a(m):
+            for t in range(4):
+                nc.sync.dma_start(
+                    out=a_raw[t:P:4, m, :],
+                    in_=A[4 * t : 4 * t + 4].rearrange("a (i m b) r -> (a i) m (b r)", i=8, m=MC, b=64)[:, m, :],
                 )
 
-        Bf = B.rearrange("k r i -> (k r) i")
-        if A_ON_GPSIMD:
-            load_a()
-        x_raw = [load_rows(x, P * i, "x_raw%d" % i) for i in range(NB)]
-        b_raw = [load_rows(Bf, P * i, "b_raw%d" % i) for i in range(4)]
-        w_raw = [load_rows(Wb, P * i, "w_raw%d" % i) for i in range(4)]
-        if not A_ON_GPSIMD:
-            load_a()
-        for i in range(4, 16):
-            w_raw.append(load_rows(Wb, P * i, "w_raw%d" % i))
+        x_raw = [load_rows(xv[c], "x_raw") for c in range(NB)]
+        b_raw = [load_rows(Bf[P * t : P * t + P, :], "b_raw") for t in range(4)]
+        w_raw = []
+        for m in range(MC):
+            for j in range(4):
+                w_raw.append(load_w(m, j))
+            load_a(m)
 
         mx = small.tile([P, NB], F32, name="mx")
         nc.vector.tensor_reduce(out=mx[:], in_=sc_b[:], axis=AX.X, op=ALU.max)
@@ -180,10 +179,16 @@ def tile_submatrixlinear_pa_kernel(tc, x, scores, Wb, bb, A, B, out):
                     stop=(g == G - 1),
                 )
 
-        def a_chunk(m):
+        def a_transpose(m):
             y = grp.tile([P, 2048], BF16, name="y", tag="y", bufs=2, align_bytes=64)
             nc.vector.transpose(out=y[:], in_=a_raw[:, m, :])
+            return y
+
+        def a_quantise(m, y):
             nc.vector.quantize_mx(out=aq[:, m, :].bitcast(FP8X4), scales=asc[:, m, :], in_=y[:])
+
+        def a_chunk(m):
+            a_quantise(m, a_transpose(m))
 
         def w_block(m, j, wg):
             words = w_raw[4 * m + j][:].bitcast(F32)
@@ -193,7 +198,7 @@ def tile_submatrixlinear_pa_kernel(tc, x, scores, Wb, bb, A, B, out):
                 for g2 in range(2):
                     for u in range(2):
                         c0 = 256 * (2 * gp + g2) + 128 * u
-                        nc.tensor.transpose(bank[:, 2 * g2 + u, :], words[:, c0 : c0 + P], perm[:])
+                        nc.tensor.transpose(bank[:, 2 * g2 + u, :], words[:, c0 : c0 + P], ident[:])
                 for g2 in range(2):
                     nc.scalar.copy(
                         out=wgw[:, j, 2 * gp + g2],
@@ -243,7 +248,7 @@ def tile_submatrixlinear_pa_kernel(tc, x, scores, Wb, bb, A, B, out):
             o = outp.tile([P, 512], F32, name="o", tag="o")
             ov = o[:].rearrange("p (i b) -> p b i", i=8)
             av = acc[:].rearrange("p (b i) -> p b i", i=8)
-            bv = bias_sb[:, 512 * m : 512 * m + 512].rearrange("p (i b) -> p b i", i=8)
+            bv = bias_sb[:].rearrange("p (i m b) -> p m b i", i=8, m=MC, b=64)[:, m]
             for i0 in range(0, 8, OUT_REGIONS):
                 nc.vector.tensor_tensor(
                     out=ov[:, :, i0 : i0 + OUT_REGIONS],
@@ -251,7 +256,7 @@ def tile_submatrixlinear_pa_kernel(tc, x, scores, Wb, bb, A, B, out):
                     in1=bv[:, :, i0 : i0 + OUT_REGIONS],
                     op=ALU.add,
                 )
-            nc.sync.dma_start(out=out[P * nb : P * nb + P, 512 * m : 512 * m + 512], in_=o[:])
+            nc.sync.dma_start(out=outv[nb, m], in_=o[:].rearrange("p (i b) -> p i b", i=8))
 
         for nb in range(NB):
             rows_to_codes(x_raw[nb], xq[:, nb], xs[:, nb])
@@ -267,20 +272,6 @@ def tile_submatrixlinear_pa_kernel(tc, x, scores, Wb, bb, A, B, out):
             )
             gts.append(gt)
 
-        for t in range(3):
-            rows_to_codes(b_raw[t], bq[:, t], bs[:, t])
-        ut = [accs.tile([P, 4, P], F32, name="ut%d" % nb, tag="acc") for nb in range(NB)]
-        for nb in range(NB):
-            ut_passes(ut, 0, nb)
-        rows_to_codes(b_raw[3], bq[:, 3], bs[:, 3])
-        wg = w_tile()
-        w_half(0, 0, wg)
-        for nb in range(NB):
-            ut_passes(ut, 1, nb)
-        for nb in range(NB):
-            ut_passes(ut, 2, nb)
-        w_half(0, 1, wg)
-
         def h_block(nb):
             nc.vector.tensor_tensor(
                 out=hg[:, nb],
@@ -289,45 +280,52 @@ def tile_submatrixlinear_pa_kernel(tc, x, scores, Wb, bb, A, B, out):
                 op=ALU.mult,
             )
 
+        for t in range(3):
+            rows_to_codes(b_raw[t], bq[:, t], bs[:, t])
+        ut = [accs.tile([P, 4, P], F32, name="ut%d" % nb, tag="acc") for nb in range(NB)]
+        for nb in range(NB):
+            ut_passes(ut, 0, nb)
+        rows_to_codes(b_raw[3], bq[:, 3], bs[:, 3])
+        for nb in range(NB):
+            ut_passes(ut, 1, nb)
+        wg = w_tile()
+        w_half(0, 0, wg)
+        for nb in range(NB):
+            ut_passes(ut, 2, nb)
+        w_half(0, 1, wg)
         for nb in range(NB):
             ut_passes(ut, 3, nb)
+        y0 = a_transpose(0)
         h_block(0)
         w_quantise(0, wg)
         for nb in range(1, NB):
             h_block(nb)
+        a_quantise(0, y0)
         nc.vector.quantize_mx(
             out=hq[:].rearrange("p c n -> p (c n)").bitcast(FP8X4),
             scales=hs[:].rearrange("p c n -> p (c n)"),
             in_=hg[:].rearrange("p c n t -> p (c n t)"),
         )
 
-        accl = [base(0, nb) for nb in range(NB)]
-        a_chunk(0)
-        wg = w_tile()
-        w_half(1, 0, wg)
-        for nb in range(NB):
-            delta(0, nb, accl[nb])
-        for nb in range(NB):
-            finish(0, nb, accl[nb])
-        w_half(1, 1, wg)
-        w_quantise(1, wg)
-        a_chunk(1)
-
-        for m in range(1, MC):
-            more = m + 1 < MC
-            if more:
-                wg = w_tile()
-                w_half(m + 1, 0, wg)
+        for m in range(MC - 1):
+            wg = w_tile()
+            w_half(m + 1, 0, wg)
             accl = [base(m, 0), base(m, 1)]
-            if more:
-                w_half(m + 1, 1, wg)
+            w_half(m + 1, 1, wg)
             accl.append(base(m, 2))
             accl.append(base(m, 3))
             for nb in range(NB):
                 delta(m, nb, accl[nb])
-            if more:
-                w_quantise(m + 1, wg)
+            w_quantise(m + 1, wg)
             for nb in range(NB):
                 finish(m, nb, accl[nb])
-            if more:
-                a_chunk(m + 1)
+            if m == 0:
+                a_chunk(1)
+                a_chunk(2)
+            if m == 1:
+                a_chunk(3)
+
+        for nb in range(NB):
+            acc = base(MC - 1, nb)
+            delta(MC - 1, nb, acc)
+            finish(MC - 1, nb, acc)

@@ -199,6 +199,8 @@ def tile_submatrixlinear_pa_kernel(tc, x, scores, Wb, bb, A, B, out):
                     for u in range(2):
                         c0 = 256 * (2 * gp + g2) + 128 * u
                         nc.tensor.transpose(bank[:, 2 * g2 + u, :], words[:, c0 : c0 + P], ident[:])
+                        if m in (1, 2):
+                            nc.tensor.transpose(bank[:, 2 * g2 + u, :], words[:, c0 : c0 + P], ident[:])
                 for g2 in range(2):
                     nc.scalar.copy(
                         out=wgw[:, j, 2 * gp + g2],

@@ -28,7 +28,6 @@ FLOPS = 2 * N_TOK * D_IN * D_OUT + 2 * N_TOK * D_IN * KR + 2 * N_TOK * KR * D_OU
 
 
 PIN = True
-OUT_REGIONS = 4
 
 
 def tile_submatrixlinear_pa_kernel(tc, x, scores, Wb, bb, A, B, out):
@@ -37,7 +36,7 @@ def tile_submatrixlinear_pa_kernel(tc, x, scores, Wb, bb, A, B, out):
         const = ctx.enter_context(tc.tile_pool(name="const", bufs=1))
         raw = ctx.enter_context(tc.tile_pool(name="raw", bufs=12))
         grp = ctx.enter_context(tc.tile_pool(name="grp", bufs=3))
-        outp = ctx.enter_context(tc.tile_pool(name="outp", bufs=8))
+        outp = ctx.enter_context(tc.tile_pool(name="outp", bufs=6))
         small = ctx.enter_context(tc.tile_pool(name="small", bufs=1))
         tps = ctx.enter_context(tc.psum_pool(name="tps", bufs=4))
         accs = ctx.enter_context(tc.psum_pool(name="accs", bufs=4))
@@ -52,7 +51,8 @@ def tile_submatrixlinear_pa_kernel(tc, x, scores, Wb, bb, A, B, out):
         nc.vector.memset(bias_row[:], 0.0)
 
         bias_sb = const.tile([P, D_OUT], F32, name="bias_sb")
-        a_raw = const.tile([P, MC, 2048], BF16, name="a_raw", align_bytes=64)
+        z0 = [const.tile([P, 8, 256], BF16, name="z0_%d" % m) for m in range(MC)]
+        gt = const.tile([P, NB, P, 2], F32, name="gt")
         xq = const.tile([P, NB, G, P], U32, name="xq", align_bytes=64)
         xs = const.tile([P, NB, G, P], U8, name="xs", align_bytes=64)
         bq = const.tile([P, 4, G, P], U32, name="bq", align_bytes=64)
@@ -66,8 +66,8 @@ def tile_submatrixlinear_pa_kernel(tc, x, scores, Wb, bb, A, B, out):
         hg = const.tile([P, NB, P, 4], BF16, name="hg", align_bytes=64)
 
         xv = x.rearrange("(p c) i -> c p i", c=NB)
-        outv = out.rearrange("(p c) (i m b) -> c m p i b", c=NB, i=8, m=MC, b=64)
-        Bf = B.rearrange("k r i -> (k r) i")
+        outv = out.rearrange("(p c) o -> c p o", c=NB)
+        Bv = B.rearrange("k r i -> (k r) i").rearrange("(u p e) i -> u e p i", u=2, e=2)
         sc_b = small.tile([P, NB, N_EXP], BF16, name="sc_b")
         nc.sync.dma_start(out=sc_b[:], in_=scores.rearrange("(p c) k -> p c k", c=NB))
         nc.sync.dma_start(out=bias_row[0:1, :], in_=bb.rearrange("(o n) -> o n", o=1))
@@ -77,26 +77,20 @@ def tile_submatrixlinear_pa_kernel(tc, x, scores, Wb, bb, A, B, out):
             nc.sync.dma_start(out=t[:], in_=src)
             return t
 
-        def load_w(m, j):
-            t = raw.tile([P, D_IN], BF16, name="w_raw", tag="raw")
-            for s in range(2):
-                r0 = 256 * (2 * j + s) + 64 * m
-                nc.sync.dma_start(out=t[s:P:2, :], in_=Wb[r0 : r0 + 64, :])
-            return t
-
         def load_a(m):
-            for t in range(4):
+            for u in range(2):
                 nc.sync.dma_start(
-                    out=a_raw[t:P:4, m, :],
-                    in_=A[4 * t : 4 * t + 4].rearrange("a (i m b) r -> (a i) m (b r)", i=8, m=MC, b=64)[:, m, :],
+                    out=z0[m][u:P:2, :, :],
+                    in_=A[8 * u : 8 * u + 8, 512 * m : 512 * m + 512, :].rearrange("k (w b) r -> w k (b r)", b=8),
                 )
 
         x_raw = [load_rows(xv[c], "x_raw") for c in range(NB)]
-        b_raw = [load_rows(Bf[P * t : P * t + P, :], "b_raw") for t in range(4)]
+        b_raw = [load_rows(Bv[t // 2, t % 2], "b_raw") for t in range(4)]
         w_raw = []
         for m in range(MC):
             for j in range(4):
-                w_raw.append(load_w(m, j))
+                r0 = 512 * m + P * j
+                w_raw.append(load_rows(Wb[r0 : r0 + P, :], "w_raw"))
             load_a(m)
 
         mx = small.tile([P, NB], F32, name="mx")
@@ -134,8 +128,8 @@ def tile_submatrixlinear_pa_kernel(tc, x, scores, Wb, bb, A, B, out):
         for nb in range(NB):
             gexp = outp.tile([P, 512], F32, name="gexp", tag="o")
             nc.vector.tensor_scalar(
-                out=gexp[:].rearrange("p (k r) -> p k r", r=RANK),
-                in0=g1[:, nb, :].unsqueeze(2).to_broadcast([P, N_EXP, RANK]),
+                out=gexp[:, 0:256].rearrange("p (k j) -> p k j", j=16),
+                in0=g1[:, nb, :].unsqueeze(2).to_broadcast([P, N_EXP, 16]),
                 scalar1=r1[:, nb : nb + 1],
                 scalar2=None,
                 op0=ALU.mult,
@@ -147,10 +141,8 @@ def tile_submatrixlinear_pa_kernel(tc, x, scores, Wb, bb, A, B, out):
             nc.tensor.matmul(out=pb[:], lhsT=ones[:], rhs=bias_row[:, 512 * m : 512 * m + 512], start=True, stop=True)
             nc.scalar.copy(out=bias_sb[:, 512 * m : 512 * m + 512], in_=pb[:])
 
-        def rows_to_codes(src, codes, scales):
+        def transpose_rows(src, dst):
             words = src[:].bitcast(F32)
-            gx = grp.tile([P, 2048], BF16, name="gx", tag="gx", align_bytes=64)
-            gxw = gx[:].bitcast(F32).rearrange("p (g n u) -> p g n u", g=G, n=P, u=2)
             for gp in range(2):
                 bank = tps.tile([P, 4, P], F32, name="bank", tag="tp")
                 for g2 in range(2):
@@ -158,9 +150,13 @@ def tile_submatrixlinear_pa_kernel(tc, x, scores, Wb, bb, A, B, out):
                         c0 = 256 * (2 * gp + g2) + 128 * u
                         nc.tensor.transpose(bank[:, 2 * g2 + u, :], words[:, c0 : c0 + P], ident[:])
                 nc.scalar.copy(
-                    out=gxw[:, 2 * gp : 2 * gp + 2],
+                    out=dst[:, 2 * gp : 2 * gp + 2],
                     in_=bank[:].rearrange("p (g u) n -> p g n u", u=2),
                 )
+
+        def rows_to_codes(src, codes, scales):
+            gx = grp.tile([P, 2048], BF16, name="gx", tag="gx", align_bytes=64)
+            transpose_rows(src, gx[:].bitcast(F32).rearrange("p (g n u) -> p g n u", g=G, n=P, u=2))
             nc.vector.quantize_mx(
                 out=codes.rearrange("p g n -> p (g n)").bitcast(FP8X4),
                 scales=scales.rearrange("p g n -> p (g n)"),
@@ -179,37 +175,33 @@ def tile_submatrixlinear_pa_kernel(tc, x, scores, Wb, bb, A, B, out):
                     stop=(g == G - 1),
                 )
 
-        def a_transpose(m):
+        def a_sort(m):
+            z1 = grp.tile([P, 2048], BF16, name="z1", tag="z1", bufs=2)
+            nc.scalar.copy(
+                out=z1[:].bitcast(F32).rearrange("p (b k w) -> p b k w", b=8, k=8, w=16),
+                in_=z0[m][:].rearrange("p k c -> p (k c)").bitcast(F32).rearrange("p (k b w) -> p b k w", k=8, b=8, w=16),
+            )
+            return z1
+
+        def a_transposes(m, z1):
             y = grp.tile([P, 2048], BF16, name="y", tag="y", bufs=2, align_bytes=64)
-            nc.vector.transpose(out=y[:], in_=a_raw[:, m, :])
+            yw = y[:].bitcast(F32).rearrange("p (w h b u) -> p h w b u", w=64, h=2, b=4, u=2)
+            zw = z1[:].bitcast(F32)
+            for h in range(2):
+                bank = tps.tile([P, 4, P], F32, name="bank", tag="tp")
+                for b in range(4):
+                    c0 = P * (4 * h + b)
+                    nc.tensor.transpose(bank[:, b, :], zw[:, c0 : c0 + P], ident[:])
+                nc.scalar.copy(out=yw[:, h], in_=bank[:].rearrange("p b (w u) -> p w b u", u=2))
             return y
 
         def a_quantise(m, y):
             nc.vector.quantize_mx(out=aq[:, m, :].bitcast(FP8X4), scales=asc[:, m, :], in_=y[:])
 
-        def a_chunk(m):
-            a_quantise(m, a_transpose(m))
-
-        def w_block(m, j, wg):
-            words = w_raw[4 * m + j][:].bitcast(F32)
-            wgw = wg[:].bitcast(F32).rearrange("p (g b j s u) -> p j g b s u", g=G, b=64, j=4, s=2, u=2)
-            for gp in range(2):
-                bank = tps.tile([P, 4, P], F32, name="bank", tag="tp")
-                for g2 in range(2):
-                    for u in range(2):
-                        c0 = 256 * (2 * gp + g2) + 128 * u
-                        nc.tensor.transpose(bank[:, 2 * g2 + u, :], words[:, c0 : c0 + P], ident[:])
-                        if m in (1, 2):
-                            nc.tensor.transpose(bank[:, 2 * g2 + u, :], words[:, c0 : c0 + P], ident[:])
-                for g2 in range(2):
-                    nc.scalar.copy(
-                        out=wgw[:, j, 2 * gp + g2],
-                        in_=bank[:, 2 * g2 : 2 * g2 + 2, :].rearrange("p u (b s) -> p b s u", s=2),
-                    )
-
         def w_half(m, half, wg):
-            w_block(m, 2 * half, wg)
-            w_block(m, 2 * half + 1, wg)
+            wgw = wg[:].bitcast(F32).rearrange("p (g j n u) -> p j g n u", g=G, j=4, n=P, u=2)
+            for j in (2 * half, 2 * half + 1):
+                transpose_rows(w_raw[4 * m + j], wgw[:, j])
 
         def w_quantise(m, wg):
             for g in range(G):
@@ -248,39 +240,26 @@ def tile_submatrixlinear_pa_kernel(tc, x, scores, Wb, bb, A, B, out):
 
         def finish(m, nb, acc):
             o = outp.tile([P, 512], F32, name="o", tag="o")
-            ov = o[:].rearrange("p (i b) -> p b i", i=8)
-            av = acc[:].rearrange("p (b i) -> p b i", i=8)
-            bv = bias_sb[:].rearrange("p (i m b) -> p m b i", i=8, m=MC, b=64)[:, m]
-            for i0 in range(0, 8, OUT_REGIONS):
-                nc.vector.tensor_tensor(
-                    out=ov[:, :, i0 : i0 + OUT_REGIONS],
-                    in0=av[:, :, i0 : i0 + OUT_REGIONS],
-                    in1=bv[:, :, i0 : i0 + OUT_REGIONS],
-                    op=ALU.add,
-                )
-            nc.sync.dma_start(out=outv[nb, m], in_=o[:].rearrange("p (i b) -> p i b", i=8))
+            nc.vector.tensor_tensor(out=o[:], in0=acc[:], in1=bias_sb[:, 512 * m : 512 * m + 512], op=ALU.add)
+            nc.sync.dma_start(out=outv[nb][:, 512 * m : 512 * m + 512], in_=o[:])
+
+        def h_block(nb):
+            nc.vector.tensor_tensor(
+                out=hg[:, nb].rearrange("p n (u e) -> p n u e", e=2),
+                in0=ut[nb][:].rearrange("p (u e) n -> p n u e", e=2),
+                in1=gt[:, nb].unsqueeze(3).to_broadcast([P, P, 2, 2]),
+                op=ALU.mult,
+            )
 
         for nb in range(NB):
             rows_to_codes(x_raw[nb], xq[:, nb], xs[:, nb])
 
-        gts = []
-        for nb in range(NB):
+        for cp in range(2):
             bank = tps.tile([P, 4, P], F32, name="bank", tag="tp")
-            for t in range(4):
-                nc.tensor.transpose(bank[:, t, :], gexps[nb][:, P * t : P * t + P], ident[:])
-            gt = outp.tile([P, 512], F32, name="gt", tag="o")
-            nc.scalar.copy(
-                out=gt[:].rearrange("p (n t) -> p n t", t=4), in_=bank[:].rearrange("p t n -> p n t")
-            )
-            gts.append(gt)
-
-        def h_block(nb):
-            nc.vector.tensor_tensor(
-                out=hg[:, nb],
-                in0=ut[nb][:].rearrange("p t n -> p n t"),
-                in1=gts[nb][:].rearrange("p (n t) -> p n t", t=4),
-                op=ALU.mult,
-            )
+            for c2 in range(2):
+                for u in range(2):
+                    nc.tensor.transpose(bank[:, 2 * c2 + u, :], gexps[2 * cp + c2][:, P * u : P * u + P], ident[:])
+            nc.scalar.copy(out=gt[:, 2 * cp : 2 * cp + 2], in_=bank[:].rearrange("p (c u) n -> p c n u", u=2))
 
         for t in range(3):
             rows_to_codes(b_raw[t], bq[:, t], bs[:, t])
@@ -295,14 +274,15 @@ def tile_submatrixlinear_pa_kernel(tc, x, scores, Wb, bb, A, B, out):
         for nb in range(NB):
             ut_passes(ut, 2, nb)
         w_half(0, 1, wg)
+        z1 = a_sort(0)
         for nb in range(NB):
             ut_passes(ut, 3, nb)
-        y0 = a_transpose(0)
+        y = a_transposes(0, z1)
         h_block(0)
         w_quantise(0, wg)
         for nb in range(1, NB):
             h_block(nb)
-        a_quantise(0, y0)
+        a_quantise(0, y)
         nc.vector.quantize_mx(
             out=hq[:].rearrange("p c n -> p (c n)").bitcast(FP8X4),
             scales=hs[:].rearrange("p c n -> p (c n)"),
@@ -316,16 +296,14 @@ def tile_submatrixlinear_pa_kernel(tc, x, scores, Wb, bb, A, B, out):
             w_half(m + 1, 1, wg)
             accl.append(base(m, 2))
             accl.append(base(m, 3))
+            z1 = a_sort(m + 1)
+            y = a_transposes(m + 1, z1)
             for nb in range(NB):
                 delta(m, nb, accl[nb])
             w_quantise(m + 1, wg)
+            a_quantise(m + 1, y)
             for nb in range(NB):
                 finish(m, nb, accl[nb])
-            if m == 0:
-                a_chunk(1)
-                a_chunk(2)
-            if m == 1:
-                a_chunk(3)
 
         for nb in range(NB):
             acc = base(MC - 1, nb)

@@ -149,10 +149,16 @@ def tile_submatrixlinear_pa_kernel(tc, x, scores, Wb, bb, A, B, out):
                     for u in range(2):
                         c0 = 256 * (2 * gp + g2) + 128 * u
                         nc.tensor.transpose(bank[:, 2 * g2 + u, :], words[:, c0 : c0 + P], ident[:])
-                nc.scalar.copy(
-                    out=dst[:, 2 * gp : 2 * gp + 2],
-                    in_=bank[:].rearrange("p (g u) n -> p g n u", u=2),
-                )
+                if gp == 0:
+                    nc.scalar.copy(
+                        out=dst[:, 2 * gp : 2 * gp + 2],
+                        in_=bank[:].rearrange("p (g u) n -> p g n u", u=2),
+                    )
+                else:
+                    nc.vector.tensor_copy(
+                        out=dst[:, 2 * gp : 2 * gp + 2],
+                        in_=bank[:].rearrange("p (g u) n -> p g n u", u=2),
+                    )
 
         def rows_to_codes(src, codes, scales):
             gx = grp.tile([P, 2048], BF16, name="gx", tag="gx", align_bytes=64)
@@ -289,9 +295,12 @@ def tile_submatrixlinear_pa_kernel(tc, x, scores, Wb, bb, A, B, out):
             in_=hg[:].rearrange("p c n t -> p (c n t)"),
         )
 
+        late = []
         for m in range(MC - 1):
             wg = w_tile()
             w_half(m + 1, 0, wg)
+            for nb, acc in late:
+                finish(m - 1, nb, acc)
             accl = [base(m, 0), base(m, 1)]
             w_half(m + 1, 1, wg)
             accl.append(base(m, 2))
@@ -302,9 +311,12 @@ def tile_submatrixlinear_pa_kernel(tc, x, scores, Wb, bb, A, B, out):
                 delta(m, nb, accl[nb])
             w_quantise(m + 1, wg)
             a_quantise(m + 1, y)
-            for nb in range(NB):
-                finish(m, nb, accl[nb])
+            finish(m, 0, accl[0])
+            finish(m, 1, accl[1])
+            late = [(2, accl[2]), (3, accl[3])]
 
+        for nb, acc in late:
+            finish(MC - 2, nb, acc)
         for nb in range(NB):
             acc = base(MC - 1, nb)
             delta(MC - 1, nb, acc)

from contextlib import ExitStack

import concourse.mybir as mybir
from concourse.masks import make_identity

F32 = mybir.dt.float32
BF16 = mybir.dt.bfloat16
U32 = mybir.dt.uint32
U8 = mybir.dt.uint8
FP8X4 = mybir.dt.float8_e4m3fn_x4
ALU = mybir.AluOpType
ACT = mybir.ActivationFunctionType
AX = mybir.AxisListType

P = 128
N_TOK = 512
D_IN = 2048
D_OUT = 2048
N_EXP = 16
RANK = 32
KR = N_EXP * RANK
NB = N_TOK // P
G = D_IN // 512
MC = D_OUT // 512
GATE_THRESHOLD = 0.05

FLOPS = 2 * N_TOK * D_IN * D_OUT + 2 * N_TOK * D_IN * KR + 2 * N_TOK * KR * D_OUT


PIN = True


def tile_submatrixlinear_pa_kernel(tc, x, scores, Wb, bb, A, B, out):
    nc = tc.nc
    with ExitStack() as ctx:
        const = ctx.enter_context(tc.tile_pool(name="const", bufs=1))
        raw = ctx.enter_context(tc.tile_pool(name="raw", bufs=12))
        grp = ctx.enter_context(tc.tile_pool(name="grp", bufs=3))
        outp = ctx.enter_context(tc.tile_pool(name="outp", bufs=6))
        small = ctx.enter_context(tc.tile_pool(name="small", bufs=1))
        tps = ctx.enter_context(tc.psum_pool(name="tps", bufs=4))
        accs = ctx.enter_context(tc.psum_pool(name="accs", bufs=4))
        if PIN:
            ctx.enter_context(tc.manual_schedule())

        ident = const.tile([P, P], F32, name="ident")
        make_identity(nc, ident[:])
        ones = const.tile([P, P], BF16, name="ones")
        nc.vector.memset(ones[:], 1.0)
        bias_row = raw.tile([P, D_OUT], BF16, name="bias_row", tag="raw")
        nc.vector.memset(bias_row[:], 0.0)

        bias_sb = const.tile([P, D_OUT], F32, name="bias_sb")
        z0 = [const.tile([P, 8, 256], BF16, name="z0_%d" % m) for m in range(MC)]
        gt = const.tile([P, NB, P, 2], F32, name="gt")
        xq = const.tile([P, NB, G, P], U32, name="xq", align_bytes=64)
        xs = const.tile([P, NB, G, P], U8, name="xs", align_bytes=64)
        bq = const.tile([P, 4, G, P], U32, name="bq", align_bytes=64)
        bs = const.tile([P, 4, G, P], U8, name="bs", align_bytes=64)
        wq = const.tile([P, MC, G, 512], U32, name="wq", align_bytes=64)
        ws = const.tile([P, MC, G, 512], U8, name="ws", align_bytes=64)
        aq = const.tile([P, MC, 512], U32, name="aq", align_bytes=64)
        asc = const.tile([P, MC, 512], U8, name="asc", align_bytes=64)
        hq = const.tile([P, NB, P], U32, name="hq", align_bytes=64)
        hs = const.tile([P, NB, P], U8, name="hs", align_bytes=64)
        hg = const.tile([P, NB, P, 4], BF16, name="hg", align_bytes=64)

        xv = x.rearrange("(p c) i -> c p i", c=NB)
        outv = out.rearrange("(p c) o -> c p o", c=NB)
        Bv = B.rearrange("k r i -> (k r) i").rearrange("(u p e) i -> u e p i", u=2, e=2)
        sc_b = small.tile([P, NB, N_EXP], BF16, name="sc_b")
        nc.sync.dma_start(out=sc_b[:], in_=scores.rearrange("(p c) k -> p c k", c=NB))
        nc.sync.dma_start(out=bias_row[0:1, :], in_=bb.rearrange("(o n) -> o n", o=1))

        def load_rows(src, nm):
            t = raw.tile([P, D_IN], BF16, name=nm, tag="raw")
            nc.sync.dma_start(out=t[:], in_=src)
            return t

        def load_a(m):
            for u in range(2):
                nc.sync.dma_start(
                    out=z0[m][u:P:2, :, :],
                    in_=A[8 * u : 8 * u + 8, 512 * m : 512 * m + 512, :].rearrange("k (w b) r -> w k (b r)", b=8),
                )

        x_raw = [load_rows(xv[c], "x_raw") for c in range(NB)]
        b_raw = [load_rows(Bv[t // 2, t % 2], "b_raw") for t in range(4)]
        w_raw = []
        for m in range(MC):
            for j in range(4):
                r0 = 512 * m + P * j
                w_raw.append(load_rows(Wb[r0 : r0 + P, :], "w_raw"))
            load_a(m)

        mx = small.tile([P, NB], F32, name="mx")
        nc.vector.tensor_reduce(out=mx[:], in_=sc_b[:], axis=AX.X, op=ALU.max)
        dif = small.tile([P, NB, N_EXP], F32, name="dif")
        nc.vector.tensor_tensor(
            out=dif[:], in0=sc_b[:], in1=mx[:].unsqueeze(2).to_broadcast([P, NB, N_EXP]), op=ALU.subtract
        )
        ex = small.tile([P, NB, N_EXP], F32, name="ex")
        nc.scalar.activation(out=ex[:], in_=dif[:], func=ACT.Exp)
        sm = small.tile([P, NB], F32, name="sm")
        nc.vector.tensor_reduce(out=sm[:], in_=ex[:], axis=AX.X, op=ALU.add)
        rs = small.tile([P, NB], F32, name="rs")
        nc.vector.reciprocal(out=rs[:], in_=sm[:])
        g0 = small.tile([P, NB, N_EXP], F32, name="g0")
        nc.vector.tensor_tensor(
            out=g0[:], in0=ex[:], in1=rs[:].unsqueeze(2).to_broadcast([P, NB, N_EXP]), op=ALU.mult
        )
        g1 = small.tile([P, NB, N_EXP], F32, name="g1")
        nc.vector.scalar_tensor_tensor(
            out=g1[:].rearrange("p c k -> p (c k)"),
            in0=g0[:].rearrange("p c k -> p (c k)"),
            scalar=GATE_THRESHOLD,
            in1=g0[:].rearrange("p c k -> p (c k)"),
            op0=ALU.is_gt,
            op1=ALU.mult,
        )
        s1 = small.tile([P, NB], F32, name="s1")
        nc.vector.tensor_reduce(out=s1[:], in_=g1[:], axis=AX.X, op=ALU.add)
        s1m = small.tile([P, NB], F32, name="s1m")
        nc.vector.tensor_scalar_max(out=s1m[:], in0=s1[:], scalar1=1e-8)
        r1 = small.tile([P, NB], F32, name="r1")
        nc.vector.reciprocal(out=r1[:], in_=s1m[:])
        gexps = []
        for nb in range(NB):
            gexp = outp.tile([P, 512], F32, name="gexp", tag="o")
            nc.vector.tensor_scalar(
                out=gexp[:, 0:256].rearrange("p (k j) -> p k j", j=16),
                in0=g1[:, nb, :].unsqueeze(2).to_broadcast([P, N_EXP, 16]),
                scalar1=r1[:, nb : nb + 1],
                scalar2=None,
                op0=ALU.mult,
            )
            gexps.append(gexp)

        for m in range(MC):
            pb = accs.tile([P, 512], F32, name="pb", tag="acc")
            nc.tensor.matmul(out=pb[:], lhsT=ones[:], rhs=bias_row[:, 512 * m : 512 * m + 512], start=True, stop=True)
            nc.scalar.copy(out=bias_sb[:, 512 * m : 512 * m + 512], in_=pb[:])

        def transpose_rows(src, dst):
            words = src[:].bitcast(F32)
            for gp in range(2):
                bank = tps.tile([P, 4, P], F32, name="bank", tag="tp")
                for g2 in range(2):
                    for u in range(2):
                        c0 = 256 * (2 * gp + g2) + 128 * u
                        nc.tensor.transpose(bank[:, 2 * g2 + u, :], words[:, c0 : c0 + P], ident[:])
                if gp == 0:
                    nc.scalar.copy(
                        out=dst[:, 2 * gp : 2 * gp + 2],
                        in_=bank[:].rearrange("p (g u) n -> p g n u", u=2),
                    )
                else:
                    nc.vector.tensor_copy(
                        out=dst[:, 2 * gp : 2 * gp + 2],
                        in_=bank[:].rearrange("p (g u) n -> p g n u", u=2),
                    )

        def rows_to_codes(src, codes, scales):
            gx = grp.tile([P, 2048], BF16, name="gx", tag="gx", align_bytes=64)
            transpose_rows(src, gx[:].bitcast(F32).rearrange("p (g n u) -> p g n u", g=G, n=P, u=2))
            nc.vector.quantize_mx(
                out=codes.rearrange("p g n -> p (g n)").bitcast(FP8X4),
                scales=scales.rearrange("p g n -> p (g n)"),
                in_=gx[:],
            )

        def ut_passes(ut, t, nb):
            for g in range(G):
                nc.tensor.matmul_mx(
                    out=ut[nb][:, t, :],
                    lhsT=bq[:, t, g, :].bitcast(FP8X4),
                    lhsT_scale=bs[:, t, g, :],
                    rhs=xq[:, nb, g, :].bitcast(FP8X4),
                    rhs_scale=xs[:, nb, g, :],
                    start=(g == 0),
                    stop=(g == G - 1),
                )

        def a_sort(m):
            z1 = grp.tile([P, 2048], BF16, name="z1", tag="z1", bufs=2)
            nc.scalar.copy(
                out=z1[:].bitcast(F32).rearrange("p (b k w) -> p b k w", b=8, k=8, w=16),
                in_=z0[m][:].rearrange("p k c -> p (k c)").bitcast(F32).rearrange("p (k b w) -> p b k w", k=8, b=8, w=16),
            )
            return z1

        def a_transposes(m, z1):
            y = grp.tile([P, 2048], BF16, name="y", tag="y", bufs=2, align_bytes=64)
            yw = y[:].bitcast(F32).rearrange("p (w h b u) -> p h w b u", w=64, h=2, b=4, u=2)
            zw = z1[:].bitcast(F32)
            for h in range(2):
                bank = tps.tile([P, 4, P], F32, name="bank", tag="tp")
                for b in range(4):
                    c0 = P * (4 * h + b)
                    nc.tensor.transpose(bank[:, b, :], zw[:, c0 : c0 + P], ident[:])
                nc.scalar.copy(out=yw[:, h], in_=bank[:].rearrange("p b (w u) -> p w b u", u=2))
            return y

        def a_quantise(m, y):
            nc.vector.quantize_mx(out=aq[:, m, :].bitcast(FP8X4), scales=asc[:, m, :], in_=y[:])

        def w_half(m, half, wg):
            wgw = wg[:].bitcast(F32).rearrange("p (g j n u) -> p j g n u", g=G, j=4, n=P, u=2)
            for j in (2 * half, 2 * half + 1):
                transpose_rows(w_raw[4 * m + j], wgw[:, j])

        def w_quantise(m, wg):
            for g in range(G):
                nc.vector.quantize_mx(
                    out=wq[:, m, g, :].bitcast(FP8X4), scales=ws[:, m, g, :], in_=wg[:, 2048 * g : 2048 * g + 2048]
                )

        def w_tile():
            wg = grp.tile([P, G * 2048], BF16, name="wg", tag="wg", bufs=2, align_bytes=64)
            return wg

        def base(m, nb):
            acc = accs.tile([P, 512], F32, name="acc", tag="acc")
            for g in range(G):
                nc.tensor.matmul_mx(
                    out=acc[:],
                    lhsT=xq[:, nb, g, :].bitcast(FP8X4),
                    lhsT_scale=xs[:, nb, g, :],
                    rhs=wq[:, m, g, :].bitcast(FP8X4),
                    rhs_scale=ws[:, m, g, :],
                    start=(g == 0),
                    stop=False,
                )
            return acc

        def delta(m, nb, acc):
            nc.tensor.matmul_mx(
                out=acc[:],
                lhsT=hq[:, nb, :].bitcast(FP8X4),
                lhsT_scale=hs[:, nb, :],
                rhs=aq[:, m, :].bitcast(FP8X4),
                rhs_scale=asc[:, m, :],
                start=False,
                stop=True,
            )

        def finish(m, nb, acc):
            o = outp.tile([P, 512], F32, name="o", tag="o")
            nc.vector.tensor_tensor(out=o[:], in0=acc[:], in1=bias_sb[:, 512 * m : 512 * m + 512], op=ALU.add)
            nc.sync.dma_start(out=outv[nb][:, 512 * m : 512 * m + 512], in_=o[:])

        def h_block(nb):
            nc.vector.tensor_tensor(
                out=hg[:, nb].rearrange("p n (u e) -> p n u e", e=2),
                in0=ut[nb][:].rearrange("p (u e) n -> p n u e", e=2),
                in1=gt[:, nb].unsqueeze(3).to_broadcast([P, P, 2, 2]),
                op=ALU.mult,
            )

        for nb in range(NB):
            rows_to_codes(x_raw[nb], xq[:, nb], xs[:, nb])

        for cp in range(2):
            bank = tps.tile([P, 4, P], F32, name="bank", tag="tp")
            for c2 in range(2):
                for u in range(2):
                    nc.tensor.transpose(bank[:, 2 * c2 + u, :], gexps[2 * cp + c2][:, P * u : P * u + P], ident[:])
            nc.scalar.copy(out=gt[:, 2 * cp : 2 * cp + 2], in_=bank[:].rearrange("p (c u) n -> p c n u", u=2))

        for t in range(3):
            rows_to_codes(b_raw[t], bq[:, t], bs[:, t])
        ut = [accs.tile([P, 4, P], F32, name="ut%d" % nb, tag="acc") for nb in range(NB)]
        for nb in range(NB):
            ut_passes(ut, 0, nb)
        rows_to_codes(b_raw[3], bq[:, 3], bs[:, 3])
        for nb in range(NB):
            ut_passes(ut, 1, nb)
        wg = w_tile()
        w_half(0, 0, wg)
        for nb in range(NB):
            ut_passes(ut, 2, nb)
        w_half(0, 1, wg)
        z1 = a_sort(0)
        for nb in range(NB):
            ut_passes(ut, 3, nb)
        y = a_transposes(0, z1)
        h_block(0)
        w_quantise(0, wg)
        for nb in range(1, NB):
            h_block(nb)
        a_quantise(0, y)
        nc.vector.quantize_mx(
            out=hq[:].rearrange("p c n -> p (c n)").bitcast(FP8X4),
            scales=hs[:].rearrange("p c n -> p (c n)"),
            in_=hg[:].rearrange("p c n t -> p (c n t)"),
        )

        late = []
        for m in range(MC - 1):
            wg = w_tile()
            w_half(m + 1, 0, wg)
            for nb, acc in late:
                finish(m - 1, nb, acc)
            accl = [base(m, 0), base(m, 1)]
            w_half(m + 1, 1, wg)
            accl.append(base(m, 2))
            accl.append(base(m, 3))
            z1 = a_sort(m + 1)
            y = a_transposes(m + 1, z1)
            for nb in range(NB):
                delta(m, nb, accl[nb])
            w_quantise(m + 1, wg)
            a_quantise(m + 1, y)
            finish(m, 0, accl[0])
            finish(m, 1, accl[1])
            late = [(2, accl[2]), (3, accl[3])]

        for nb, acc in late:
            finish(MC - 2, nb, acc)
        for nb in range(NB):
            acc = base(MC - 1, nb)
            delta(MC - 1, nb, acc)
            finish(MC - 1, nb, acc)
